import numpy as np
import ml_dtypes

BF16 = ml_dtypes.bfloat16


def bf(x):
    return np.asarray(x, np.float32).astype(BF16)


def f32(x):
    return np.asarray(x, np.float32)


def f64(x):
    return np.asarray(x).astype(np.float64)


def striped(idx):
    return np.tile(idx.reshape(-1, 16).T, (8, 1))


H, D, S, N, H3, NODES, BS = 256, 128, 4096, 512, 768, 4, 128
PARTS, PHASES, T_STEP = 3, 8, 5


def sigmoid(v):
    return 1.0 / (1.0 + np.exp(-v))


def clock_mask():
    phase = (PHASES * np.arange(H)) // (H - 1) + 1
    return ((T_STEP + 1) % phase == 0)[:, None]


def mix(a, p):
    q = p.reshape(H3, NODES, BS)
    return (a[None, :, :, None] * q[:, None, :, :]).sum(axis=2).reshape(H3, N)


def setup_inputs():
    return {"base": f32(np.random.standard_normal((H, S))), "x": bf(np.random.standard_normal((D, N))), "hx": bf(np.random.standard_normal((H, N))), "w_ih": bf(np.random.standard_normal((D, H3)) / np.sqrt(D)), "w_hh": bf(np.random.standard_normal((H, H3)) / np.sqrt(H)), "b_ih": f32(0.5 * np.random.standard_normal((H3, 1))), "b_hh": f32(0.5 * np.random.standard_normal((H3, 1))), "infl": f32(np.random.uniform(0.1, 1.0, (NODES, NODES))), "cmask": f32(clock_mask()), "offs": striped(np.random.permutation(S)[:N])}


def reference(base, x, hx, w_ih, w_hh, b_ih, b_hh, infl, cmask, offs):
    idx = offs[:16].T.reshape(-1)
    h = f64(hx)
    cm = f64(cmask)
    a = f64(infl) / f64(infl).sum(axis=1, keepdims=True)
    i_r, i_z, i_n = np.split(mix(a, f64(w_ih).T @ f64(x) + f64(b_ih)), PARTS)
    h_r, h_z, h_n = np.split(mix(a, f64(w_hh).T @ h + f64(b_hh)), PARTS)
    r = sigmoid(i_r + h_r)
    z = sigmoid(i_z + h_z)
    n = np.tanh(i_n + r * h_n)
    hy = n - n * z + z * h
    out = f64(base).copy()
    out[:, idx] = cm * hy + (1.0 - cm) * h
    return out

@@ -1,0 +1,148 @@
+import concourse.mybir as mybir
+from concourse.masks import make_identity
+
+F32 = mybir.dt.float32
+BF16 = mybir.dt.bfloat16
+U16 = mybir.dt.uint16
+ALU = mybir.AluOpType
+FUNC = mybir.ActivationFunctionType
+
+P = 128
+H, D = 256, 128
+S, N = 4096, 512
+NODES = 4
+BLOCKS = H // P
+PIECES = N // P
+GROUP = P // NODES
+
+FLOPS = 2 * (D + H) * 3 * H * N + 2 * NODES * 2 * 3 * H * N
+
+
+def piece(ap, s):
+    return ap.rearrange("k (m s) -> k s m", s=PIECES)[:, s, :]
+
+
+def tile_staticgraphgrucell_kernel(
+    tc, base, x, hx, w_ih, w_hh, b_ih, b_hh, infl, cmask, offs, out
+):
+    nc = tc.nc
+    with (
+        tc.tile_pool(name="held", bufs=1) as held,
+        tc.tile_pool(name="work", bufs=2) as work,
+        tc.psum_pool(name="proj", bufs=4) as proj,
+        tc.psum_pool(name="mix", bufs=1) as mix,
+    ):
+        offsets = held.tile([P, N // 16], U16, name="offsets")
+        nc.sync.dma_start(offsets[:], offs)
+        x_sb = held.tile([D, N], BF16, name="x_sb")
+        nc.sync.dma_start(x_sb[:], x)
+        w_ih_sb = held.tile([D, 3 * H], BF16, name="w_ih_sb")
+        nc.sync.dma_start(w_ih_sb[:], w_ih)
+        hx_sb = [held.tile([P, N], BF16, name=f"hx_sb{b}") for b in range(BLOCKS)]
+        w_hh_sb = [held.tile([P, 3 * H], BF16, name=f"w_hh_sb{b}") for b in range(BLOCKS)]
+        for b in range(BLOCKS):
+            nc.scalar.dma_start(hx_sb[b][:], hx[b * P : (b + 1) * P, :])
+            nc.scalar.dma_start(w_hh_sb[b][:], w_hh[b * P : (b + 1) * P, :])
+        window = [held.tile([P, S], F32, name=f"window{b}") for b in range(BLOCKS)]
+        nc.sync.dma_start(window[0][:], base[0:P, :])
+        nc.scalar.dma_start(window[1][:], base[P : 2 * P, :])
+
+        identity = held.tile([P, P], F32, name="identity")
+        make_identity(nc, identity[:])
+        rows = held.tile([P, P], F32, name="rows")
+        nc.gpsimd.memset(rows[:], 0.0)
+        nc.gpsimd.dma_start(rows[0:6, :], b_ih.rearrange("(k p) one -> k (p one)", p=P))
+        nc.gpsimd.dma_start(rows[6:12, :], b_hh.rearrange("(k p) one -> k (p one)", p=P))
+        nc.gpsimd.dma_start(rows[12:14, :], cmask.rearrange("(k p) one -> k (p one)", p=P))
+        cols_ps = proj.tile([P, N], F32, tag="proj", name="cols_ps")
+        nc.tensor.transpose(cols_ps[:, 0:P], rows[:], identity[:])
+        cols = held.tile([P, 14], F32, name="cols")
+        nc.vector.tensor_copy(cols[:], cols_ps[:, 0:14])
+        bias_rz = held.tile([P, 4], F32, name="bias_rz")
+        nc.vector.tensor_tensor(bias_rz[:], cols[:, 0:4], cols[:, 6:10], ALU.add)
+        one_minus_cm = held.tile([P, BLOCKS], F32, name="one_minus_cm")
+        nc.vector.tensor_scalar(one_minus_cm[:], cols[:, 12:14], -1.0, 1.0, ALU.mult, ALU.add)
+
+        infl_sb = held.tile([P, NODES, NODES], F32, name="infl_sb")
+        nc.gpsimd.dma_start(
+            infl_sb[:].rearrange("p v u -> p (v u)"),
+            infl.rearrange("v u -> (v u)").partition_broadcast(P),
+        )
+        row_sum = held.tile([P, NODES], F32, name="row_sum")
+        nc.vector.reduce_sum(row_sum[:], infl_sb[:], axis=mybir.AxisListType.X)
+        row_inv = held.tile([P, NODES], F32, name="row_inv")
+        nc.vector.reciprocal(row_inv[:], row_sum[:])
+        a_sb = held.tile([P, NODES, NODES], F32, name="a_sb")
+        nc.vector.tensor_tensor(
+            a_sb[:], infl_sb[:], row_inv[:].unsqueeze(2).to_broadcast([P, NODES, NODES]), ALU.mult
+        )
+        mixer = held.tile([P, NODES, GROUP], F32, name="mixer")
+        for u in range(NODES):
+            part = slice(u * GROUP, (u + 1) * GROUP)
+            nc.vector.tensor_tensor(
+                mixer[part, :, :],
+                identity[part, part].unsqueeze(1).to_broadcast([GROUP, NODES, GROUP]),
+                a_sb[part, :, u : u + 1].to_broadcast([GROUP, NODES, GROUP]),
+                ALU.mult,
+            )
+        mixer_2d = mixer[:].rearrange("p v k -> p (v k)")
+
+        rz_sb = [held.tile([P, 2 * H], F32, name=f"rz_sb{s}") for s in range(PIECES)]
+        n_sb = [held.tile([P, 2 * H], F32, name=f"n_sb{s}") for s in range(PIECES)]
+        for s in range(PIECES):
+            x_s = piece(x_sb[:], s)
+            h_s = [piece(hx_sb[b][:], s) for b in range(BLOCKS)]
+            rz_ps = proj.tile([P, 2 * H], F32, tag="proj", name="rz_ps")
+            nc.tensor.matmul(rz_ps[:], x_s, w_ih_sb[:, 0 : 2 * H], start=True, stop=False)
+            nc.tensor.matmul(rz_ps[:], h_s[0], w_hh_sb[0][:, 0 : 2 * H], start=False, stop=False)
+            nc.tensor.matmul(rz_ps[:], h_s[1], w_hh_sb[1][:, 0 : 2 * H], start=False, stop=True)
+            nc.scalar.copy(rz_sb[s][:], rz_ps[:])
+            n_ps = proj.tile([P, 2 * H], F32, tag="proj", name="n_ps")
+            nc.tensor.matmul(n_ps[:, 0:H], x_s, w_ih_sb[:, 2 * H : 3 * H], start=True, stop=True)
+            nc.tensor.matmul(n_ps[:, H : 2 * H], h_s[0], w_hh_sb[0][:, 2 * H : 3 * H], start=True, stop=False)
+            nc.tensor.matmul(n_ps[:, H : 2 * H], h_s[1], w_hh_sb[1][:, 2 * H : 3 * H], start=False, stop=True)
+            nc.vector.tensor_copy(n_sb[s][:], n_ps[:])
+
+        def mixed(name, pieces, first):
+            m_ps = mix.tile([P, N], F32, tag=name, name=name)
+            for s in range(PIECES):
+                nc.tensor.matmul(
+                    piece(m_ps[:], s), pieces[s][:, first : first + P], mixer_2d, start=True, stop=True
+                )
+            return m_ps
+
+        for b in range(BLOCKS):
+            cm = cols[:, 12 + b : 13 + b]
+            kept = work.tile([P, N], F32, name="kept")
+            nc.gpsimd.tensor_scalar(kept[:], hx_sb[b][:], one_minus_cm[:, b : b + 1], 0.0, ALU.mult, ALU.add)
+
+            m_r = mixed("m_r", rz_sb, b * P)
+            r = work.tile([P, N], F32, name="r")
+            nc.scalar.activation(r[:], m_r[:], FUNC.Sigmoid, bias=bias_rz[:, b : b + 1])
+
+            m_hn = mixed("m_hn", n_sb, H + b * P)
+            r_hn = work.tile([P, N], F32, name="r_hn")
+            nc.vector.scalar_tensor_tensor(
+                r_hn[:], m_hn[:], cols[:, 10 + b : 11 + b], r[:], ALU.add, ALU.mult
+            )
+            m_in = mixed("m_in", n_sb, b * P)
+            pre_n = work.tile([P, N], F32, name="pre_n")
+            nc.vector.tensor_tensor(pre_n[:], r_hn[:], m_in[:], ALU.add)
+            n = work.tile([P, N], F32, name="n")
+            nc.scalar.activation(n[:], pre_n[:], FUNC.Tanh, bias=cols[:, 4 + b : 5 + b])
+
+            m_z = mixed("m_z", rz_sb, H + b * P)
+            z = work.tile([P, N], F32, name="z")
+            nc.scalar.activation(z[:], m_z[:], FUNC.Sigmoid, bias=bias_rz[:, 2 + b : 3 + b])
+
+            h_minus_n = work.tile([P, N], F32, name="h_minus_n")
+            nc.vector.tensor_tensor(h_minus_n[:], hx_sb[b][:], n[:], ALU.subtract)
+            step = work.tile([P, N], F32, name="step")
+            nc.vector.tensor_tensor(step[:], z[:], h_minus_n[:], ALU.mult)
+            hy = work.tile([P, N], F32, name="hy")
+            nc.vector.tensor_tensor(hy[:], step[:], n[:], ALU.add)
+            renewed = work.tile([P, N], F32, name="renewed")
+            nc.vector.tensor_scalar(renewed[:], hy[:], cm, None, ALU.mult)
+
+            nc.vector.tensor_tensor(window[b][:].indirect(offsets[:]), renewed[:], kept[:], ALU.add)
+            nc.sync.dma_start(out[b * P : (b + 1) * P, :], window[b][:])

@@ -11,15 +11,20 @@ P = 128
 H, D = 256, 128
 S, N = 4096, 512
 NODES = 4
+GATES = 3
 BLOCKS = H // P
 PIECES = N // P
 GROUP = P // NODES
 
-FLOPS = 2 * (D + H) * 3 * H * N + 2 * NODES * 2 * 3 * H * N
+FLOPS = 2 * (D + H) * GATES * H * N + 2 * NODES * 2 * GATES * H * N
 
 
-def piece(ap, s):
+def every_fourth(ap, s):
     return ap.rearrange("k (m s) -> k s m", s=PIECES)[:, s, :]
+
+
+def gates_of_block(w, b):
+    return w.rearrange("k (g b c) -> k b g c", g=GATES, b=BLOCKS)[:, b, :, :]
 
 
 def tile_staticgraphgrucell_kernel(
@@ -32,42 +37,35 @@ def tile_staticgraphgrucell_kernel(
         tc.psum_pool(name="proj", bufs=4) as proj,
         tc.psum_pool(name="mix", bufs=1) as mix,
     ):
+        infl_sb = held.tile([P, NODES, NODES], F32, name="infl_sb")
+        nc.sync.dma_start(
+            infl_sb[:].rearrange("p v u -> p (v u)"),
+            infl.rearrange("v u -> (v u)").partition_broadcast(P),
+        )
+        hx_sb = [held.tile([P, N], BF16, name=f"hx_sb{k}") for k in range(BLOCKS)]
+        w_hh_sb = [held.tile([P, GATES * H], BF16, name=f"w_hh_sb{k}") for k in range(BLOCKS)]
+        x_sb = held.tile([D, N], BF16, name="x_sb")
+        w_ih_sb = held.tile([D, GATES * H], BF16, name="w_ih_sb")
+        nc.sync.dma_start(hx_sb[0][:], hx[0:P, :])
+        nc.scalar.dma_start(hx_sb[1][:], hx[P : 2 * P, :])
+        nc.sync.dma_start(w_hh_sb[0][:], w_hh[0:P, :])
+        nc.scalar.dma_start(w_hh_sb[1][:], w_hh[P : 2 * P, :])
+        nc.sync.dma_start(x_sb[:], x)
+        nc.scalar.dma_start(w_ih_sb[:], w_ih)
         offsets = held.tile([P, N // 16], U16, name="offsets")
         nc.sync.dma_start(offsets[:], offs)
-        x_sb = held.tile([D, N], BF16, name="x_sb")
-        nc.sync.dma_start(x_sb[:], x)
-        w_ih_sb = held.tile([D, 3 * H], BF16, name="w_ih_sb")
-        nc.sync.dma_start(w_ih_sb[:], w_ih)
-        hx_sb = [held.tile([P, N], BF16, name=f"hx_sb{b}") for b in range(BLOCKS)]
-        w_hh_sb = [held.tile([P, 3 * H], BF16, name=f"w_hh_sb{b}") for b in range(BLOCKS)]
-        for b in range(BLOCKS):
-            nc.scalar.dma_start(hx_sb[b][:], hx[b * P : (b + 1) * P, :])
-            nc.scalar.dma_start(w_hh_sb[b][:], w_hh[b * P : (b + 1) * P, :])
         window = [held.tile([P, S], F32, name=f"window{b}") for b in range(BLOCKS)]
-        nc.sync.dma_start(window[0][:], base[0:P, :])
-        nc.scalar.dma_start(window[1][:], base[P : 2 * P, :])
+        for b in range(BLOCKS):
+            nc.sync.dma_start(window[b][:], base[b * P : (b + 1) * P, :])
 
-        identity = held.tile([P, P], F32, name="identity")
-        make_identity(nc, identity[:])
         rows = held.tile([P, P], F32, name="rows")
         nc.gpsimd.memset(rows[:], 0.0)
         nc.gpsimd.dma_start(rows[0:6, :], b_ih.rearrange("(k p) one -> k (p one)", p=P))
         nc.gpsimd.dma_start(rows[6:12, :], b_hh.rearrange("(k p) one -> k (p one)", p=P))
         nc.gpsimd.dma_start(rows[12:14, :], cmask.rearrange("(k p) one -> k (p one)", p=P))
-        cols_ps = proj.tile([P, N], F32, tag="proj", name="cols_ps")
-        nc.tensor.transpose(cols_ps[:, 0:P], rows[:], identity[:])
-        cols = held.tile([P, 14], F32, name="cols")
-        nc.vector.tensor_copy(cols[:], cols_ps[:, 0:14])
-        bias_rz = held.tile([P, 4], F32, name="bias_rz")
-        nc.vector.tensor_tensor(bias_rz[:], cols[:, 0:4], cols[:, 6:10], ALU.add)
-        one_minus_cm = held.tile([P, BLOCKS], F32, name="one_minus_cm")
-        nc.vector.tensor_scalar(one_minus_cm[:], cols[:, 12:14], -1.0, 1.0, ALU.mult, ALU.add)
+        identity = held.tile([P, P], F32, name="identity")
+        make_identity(nc, identity[:])
 
-        infl_sb = held.tile([P, NODES, NODES], F32, name="infl_sb")
-        nc.gpsimd.dma_start(
-            infl_sb[:].rearrange("p v u -> p (v u)"),
-            infl.rearrange("v u -> (v u)").partition_broadcast(P),
-        )
         row_sum = held.tile([P, NODES], F32, name="row_sum")
         nc.vector.reduce_sum(row_sum[:], infl_sb[:], axis=mybir.AxisListType.X)
         row_inv = held.tile([P, NODES], F32, name="row_inv")
@@ -87,62 +85,90 @@ def tile_staticgraphgrucell_kernel(
             )
         mixer_2d = mixer[:].rearrange("p v k -> p (v k)")
 
-        rz_sb = [held.tile([P, 2 * H], F32, name=f"rz_sb{s}") for s in range(PIECES)]
-        n_sb = [held.tile([P, 2 * H], F32, name=f"n_sb{s}") for s in range(PIECES)]
-        for s in range(PIECES):
-            x_s = piece(x_sb[:], s)
-            h_s = [piece(hx_sb[b][:], s) for b in range(BLOCKS)]
-            rz_ps = proj.tile([P, 2 * H], F32, tag="proj", name="rz_ps")
-            nc.tensor.matmul(rz_ps[:], x_s, w_ih_sb[:, 0 : 2 * H], start=True, stop=False)
-            nc.tensor.matmul(rz_ps[:], h_s[0], w_hh_sb[0][:, 0 : 2 * H], start=False, stop=False)
-            nc.tensor.matmul(rz_ps[:], h_s[1], w_hh_sb[1][:, 0 : 2 * H], start=False, stop=True)
-            nc.scalar.copy(rz_sb[s][:], rz_ps[:])
-            n_ps = proj.tile([P, 2 * H], F32, tag="proj", name="n_ps")
-            nc.tensor.matmul(n_ps[:, 0:H], x_s, w_ih_sb[:, 2 * H : 3 * H], start=True, stop=True)
-            nc.tensor.matmul(n_ps[:, H : 2 * H], h_s[0], w_hh_sb[0][:, 2 * H : 3 * H], start=True, stop=False)
-            nc.tensor.matmul(n_ps[:, H : 2 * H], h_s[1], w_hh_sb[1][:, 2 * H : 3 * H], start=False, stop=True)
-            nc.vector.tensor_copy(n_sb[s][:], n_ps[:])
+        def project(b):
+            pieces = []
+            for s in range(PIECES):
+                x_s = every_fourth(x_sb[:], s)
+                pt_ps = proj.tile([P, 4 * P], F32, name="pt_ps")
+                r_z_hn = pt_ps[:, 0 : 3 * P].rearrange("m (g c) -> m g c", g=GATES)
+                for k in range(BLOCKS):
+                    nc.tensor.matmul(
+                        r_z_hn, every_fourth(hx_sb[k][:], s), gates_of_block(w_hh_sb[k][:], b),
+                        start=(k == 0), stop=False,
+                    )
+                nc.tensor.matmul(
+                    r_z_hn[:, 0:2, :], x_s, gates_of_block(w_ih_sb[:], b)[:, 0:2, :], start=False, stop=True
+                )
+                nc.tensor.matmul(
+                    pt_ps[:, 3 * P : 4 * P], x_s, gates_of_block(w_ih_sb[:], b)[:, 2, :], start=True, stop=True
+                )
+                pt_sb = held.tile([P, 4 * P], F32, name=f"pt_sb{b}{s}")
+                if b == 0 and s % 2 == 1:
+                    nc.vector.tensor_copy(pt_sb[:], pt_ps[:])
+                else:
+                    nc.scalar.copy(pt_sb[:], pt_ps[:])
+                pieces.append(pt_sb)
+            return pieces
 
-        def mixed(name, pieces, first):
+        def mixed(name, pieces, q):
             m_ps = mix.tile([P, N], F32, tag=name, name=name)
             for s in range(PIECES):
                 nc.tensor.matmul(
-                    piece(m_ps[:], s), pieces[s][:, first : first + P], mixer_2d, start=True, stop=True
+                    every_fourth(m_ps[:], s), pieces[s][:, q * P : (q + 1) * P], mixer_2d, start=True, stop=True
                 )
             return m_ps
 
+        pieces = project(0)
+
+        cols_ps = proj.tile([P, 4 * P], F32, tag="pt_ps", name="cols_ps")
+        nc.tensor.transpose(cols_ps[:, 0:P], rows[:], identity[:])
+        cols = held.tile([P, 14], F32, name="cols")
+        nc.vector.tensor_copy(cols[:], cols_ps[:, 0:14])
+        bias_r = held.tile([P, BLOCKS], F32, name="bias_r")
+        nc.vector.tensor_tensor(bias_r[:], cols[:, 0:2], cols[:, 6:8], ALU.add)
+        neg_bias_z = held.tile([P, BLOCKS], F32, name="neg_bias_z")
+        nc.vector.scalar_tensor_tensor(
+            neg_bias_z[:], cols[:, 2:4], -1.0, cols[:, 8:10], ALU.mult, ALU.subtract
+        )
+        one_minus_cm = held.tile([P, BLOCKS], F32, name="one_minus_cm")
+        nc.vector.tensor_scalar(one_minus_cm[:], cols[:, 12:14], -1.0, 1.0, ALU.mult, ALU.add)
+
         for b in range(BLOCKS):
             cm = cols[:, 12 + b : 13 + b]
+            masked_h = work.tile([P, N], F32, name="masked_h")
+            nc.gpsimd.tensor_scalar(masked_h[:], hx_sb[b][:], cm, 0.0, ALU.mult, ALU.add)
             kept = work.tile([P, N], F32, name="kept")
             nc.gpsimd.tensor_scalar(kept[:], hx_sb[b][:], one_minus_cm[:, b : b + 1], 0.0, ALU.mult, ALU.add)
 
-            m_r = mixed("m_r", rz_sb, b * P)
+            m_r = mixed("m_r", pieces, 0)
             r = work.tile([P, N], F32, name="r")
-            nc.scalar.activation(r[:], m_r[:], FUNC.Sigmoid, bias=bias_rz[:, b : b + 1])
+            nc.scalar.activation(r[:], m_r[:], FUNC.Sigmoid, bias=bias_r[:, b : b + 1])
 
-            m_hn = mixed("m_hn", n_sb, H + b * P)
+            m_hn = mixed("m_hn", pieces, 2)
             r_hn = work.tile([P, N], F32, name="r_hn")
             nc.vector.scalar_tensor_tensor(
                 r_hn[:], m_hn[:], cols[:, 10 + b : 11 + b], r[:], ALU.add, ALU.mult
             )
-            m_in = mixed("m_in", n_sb, b * P)
+            m_in = mixed("m_in", pieces, 3)
             pre_n = work.tile([P, N], F32, name="pre_n")
             nc.vector.tensor_tensor(pre_n[:], r_hn[:], m_in[:], ALU.add)
             n = work.tile([P, N], F32, name="n")
             nc.scalar.activation(n[:], pre_n[:], FUNC.Tanh, bias=cols[:, 4 + b : 5 + b])
 
-            m_z = mixed("m_z", rz_sb, H + b * P)
-            z = work.tile([P, N], F32, name="z")
-            nc.scalar.activation(z[:], m_z[:], FUNC.Sigmoid, bias=bias_rz[:, 2 + b : 3 + b])
+            gap = work.tile([P, N], F32, name="gap")
+            nc.vector.scalar_tensor_tensor(gap[:], n[:], cm, masked_h[:], ALU.mult, ALU.subtract)
+            m_z = mixed("m_z", pieces, 1)
+            one_minus_z = work.tile([P, N], F32, name="one_minus_z")
+            nc.scalar.activation(
+                one_minus_z[:], m_z[:], FUNC.Sigmoid, bias=neg_bias_z[:, b : b + 1], scale=-1.0
+            )
+            if b + 1 < BLOCKS:
+                pieces = project(b + 1)
 
-            h_minus_n = work.tile([P, N], F32, name="h_minus_n")
-            nc.vector.tensor_tensor(h_minus_n[:], hx_sb[b][:], n[:], ALU.subtract)
-            step = work.tile([P, N], F32, name="step")
-            nc.vector.tensor_tensor(step[:], z[:], h_minus_n[:], ALU.mult)
-            hy = work.tile([P, N], F32, name="hy")
-            nc.vector.tensor_tensor(hy[:], step[:], n[:], ALU.add)
+            moved = work.tile([P, N], F32, name="moved")
+            nc.vector.tensor_tensor(moved[:], gap[:], one_minus_z[:], ALU.mult)
             renewed = work.tile([P, N], F32, name="renewed")
-            nc.vector.tensor_scalar(renewed[:], hy[:], cm, None, ALU.mult)
+            nc.vector.tensor_tensor(renewed[:], moved[:], masked_h[:], ALU.add)
 
             nc.vector.tensor_tensor(window[b][:].indirect(offsets[:]), renewed[:], kept[:], ALU.add)
             nc.sync.dma_start(out[b * P : (b + 1) * P, :], window[b][:])

@@ -15,6 +15,9 @@ GATES = 3
 BLOCKS = H // P
 PIECES = N // P
 GROUP = P // NODES
+WARM_UP = 4
+QUARTER = {"r": 0, "z": 1, "hn": 2, "in": 3}
+ROWS = 14
 
 FLOPS = 2 * (D + H) * GATES * H * N + 2 * NODES * 2 * GATES * H * N
 
@@ -37,34 +40,39 @@ def tile_staticgraphgrucell_kernel(
         tc.psum_pool(name="proj", bufs=4) as proj,
         tc.psum_pool(name="mix", bufs=1) as mix,
     ):
+        hx_sb = held.tile([P, BLOCKS, N], BF16, name="hx_sb")
+        nc.sync.dma_start(hx_sb[:], hx.rearrange("(k p) j -> p k j", p=P))
+        w_hh_sb = held.tile([P, BLOCKS, GATES * H], BF16, name="w_hh_sb")
+        nc.scalar.dma_start(w_hh_sb[:], w_hh.rearrange("(k p) o -> p k o", p=P))
+        x_sb = held.tile([D, N], BF16, name="x_sb")
+        nc.sync.dma_start(x_sb[:], x)
+        w_ih_sb = held.tile([D, GATES * H], BF16, name="w_ih_sb")
+        nc.scalar.dma_start(w_ih_sb[:], w_ih)
+
         infl_sb = held.tile([P, NODES, NODES], F32, name="infl_sb")
         nc.sync.dma_start(
             infl_sb[:].rearrange("p v u -> p (v u)"),
             infl.rearrange("v u -> (v u)").partition_broadcast(P),
         )
-        hx_sb = [held.tile([P, N], BF16, name=f"hx_sb{k}") for k in range(BLOCKS)]
-        w_hh_sb = [held.tile([P, GATES * H], BF16, name=f"w_hh_sb{k}") for k in range(BLOCKS)]
-        x_sb = held.tile([D, N], BF16, name="x_sb")
-        w_ih_sb = held.tile([D, GATES * H], BF16, name="w_ih_sb")
-        nc.sync.dma_start(hx_sb[0][:], hx[0:P, :])
-        nc.scalar.dma_start(hx_sb[1][:], hx[P : 2 * P, :])
-        nc.sync.dma_start(w_hh_sb[0][:], w_hh[0:P, :])
-        nc.scalar.dma_start(w_hh_sb[1][:], w_hh[P : 2 * P, :])
-        nc.sync.dma_start(x_sb[:], x)
-        nc.scalar.dma_start(w_ih_sb[:], w_ih)
+        rows = held.tile([ROWS, P], F32, name="rows")
+        nc.gpsimd.dma_start(rows[12:14, :], cmask.rearrange("(k p) one -> k (p one)", p=P))
+        nc.sync.dma_start(rows[0:6, :], b_ih.rearrange("(k p) one -> k (p one)", p=P))
+        nc.sync.dma_start(rows[6:12, :], b_hh.rearrange("(k p) one -> k (p one)", p=P))
         offsets = held.tile([P, N // 16], U16, name="offsets")
         nc.sync.dma_start(offsets[:], offs)
         window = [held.tile([P, S], F32, name=f"window{b}") for b in range(BLOCKS)]
         for b in range(BLOCKS):
             nc.sync.dma_start(window[b][:], base[b * P : (b + 1) * P, :])
-
-        rows = held.tile([P, P], F32, name="rows")
-        nc.gpsimd.memset(rows[:], 0.0)
-        nc.gpsimd.dma_start(rows[0:6, :], b_ih.rearrange("(k p) one -> k (p one)", p=P))
-        nc.gpsimd.dma_start(rows[6:12, :], b_hh.rearrange("(k p) one -> k (p one)", p=P))
-        nc.gpsimd.dma_start(rows[12:14, :], cmask.rearrange("(k p) one -> k (p one)", p=P))
         identity = held.tile([P, P], F32, name="identity")
         make_identity(nc, identity[:])
+
+        zeros = held.tile([P, N], BF16, name="zeros")
+        nc.vector.memset(zeros[:], 0.0)
+        idle_ps = proj.tile([P, 4 * P], F32, tag="pt_ps", name="idle_ps")
+        for i in range(WARM_UP):
+            nc.tensor.matmul(idle_ps[:], zeros[:, 0:P], zeros[:], start=True, stop=True)
+        idle_sb = held.tile([P, 1], F32, name="idle_sb")
+        nc.scalar.activation(idle_sb[:], zeros[:, 0:1], FUNC.Sigmoid)
 
         row_sum = held.tile([P, NODES], F32, name="row_sum")
         nc.vector.reduce_sum(row_sum[:], infl_sb[:], axis=mybir.AxisListType.X)
@@ -93,7 +101,7 @@ def tile_staticgraphgrucell_kernel(
                 r_z_hn = pt_ps[:, 0 : 3 * P].rearrange("m (g c) -> m g c", g=GATES)
                 for k in range(BLOCKS):
                     nc.tensor.matmul(
-                        r_z_hn, every_fourth(hx_sb[k][:], s), gates_of_block(w_hh_sb[k][:], b),
+                        r_z_hn, every_fourth(hx_sb[:, k, :], s), gates_of_block(w_hh_sb[:, k, :], b),
                         start=(k == 0), stop=False,
                     )
                 nc.tensor.matmul(
@@ -110,65 +118,66 @@ def tile_staticgraphgrucell_kernel(
                 pieces.append(pt_sb)
             return pieces
 
-        def mixed(name, pieces, q):
-            m_ps = mix.tile([P, N], F32, tag=name, name=name)
+        def mixed(pieces, quarters):
+            m_ps = [mix.tile([P, N], F32, tag=f"m_{q}", name=f"m_{q}") for q in quarters]
             for s in range(PIECES):
-                nc.tensor.matmul(
-                    every_fourth(m_ps[:], s), pieces[s][:, q * P : (q + 1) * P], mixer_2d, start=True, stop=True
-                )
+                for m, q in zip(m_ps, quarters):
+                    first = QUARTER[q] * P
+                    nc.tensor.matmul(
+                        every_fourth(m[:], s), pieces[s][:, first : first + P], mixer_2d, start=True, stop=True
+                    )
             return m_ps
 
         pieces = project(0)
 
         cols_ps = proj.tile([P, 4 * P], F32, tag="pt_ps", name="cols_ps")
-        nc.tensor.transpose(cols_ps[:, 0:P], rows[:], identity[:])
-        cols = held.tile([P, 14], F32, name="cols")
-        nc.vector.tensor_copy(cols[:], cols_ps[:, 0:14])
-        bias_r = held.tile([P, BLOCKS], F32, name="bias_r")
-        nc.vector.tensor_tensor(bias_r[:], cols[:, 0:2], cols[:, 6:8], ALU.add)
-        neg_bias_z = held.tile([P, BLOCKS], F32, name="neg_bias_z")
-        nc.vector.scalar_tensor_tensor(
-            neg_bias_z[:], cols[:, 2:4], -1.0, cols[:, 8:10], ALU.mult, ALU.subtract
-        )
+        nc.tensor.matmul(cols_ps[:, 0:ROWS], rows[:], identity[0:ROWS, 0:ROWS], start=True, stop=True)
+        cols = held.tile([P, ROWS], F32, name="cols")
+        nc.vector.tensor_copy(cols[:], cols_ps[:, 0:ROWS])
+        bias_rz = held.tile([P, 2 * BLOCKS], F32, name="bias_rz")
+        nc.vector.tensor_tensor(bias_rz[:], cols[:, 0:4], cols[:, 6:10], ALU.add)
+        neg_cm = held.tile([P, BLOCKS], F32, name="neg_cm")
+        nc.vector.tensor_scalar(neg_cm[:], cols[:, 12:14], -1.0, None, ALU.mult)
         one_minus_cm = held.tile([P, BLOCKS], F32, name="one_minus_cm")
         nc.vector.tensor_scalar(one_minus_cm[:], cols[:, 12:14], -1.0, 1.0, ALU.mult, ALU.add)
 
         for b in range(BLOCKS):
             cm = cols[:, 12 + b : 13 + b]
             masked_h = work.tile([P, N], F32, name="masked_h")
-            nc.gpsimd.tensor_scalar(masked_h[:], hx_sb[b][:], cm, 0.0, ALU.mult, ALU.add)
+            nc.gpsimd.tensor_scalar(masked_h[:], hx_sb[:, b, :], cm, 0.0, ALU.mult, ALU.add)
             kept = work.tile([P, N], F32, name="kept")
-            nc.gpsimd.tensor_scalar(kept[:], hx_sb[b][:], one_minus_cm[:, b : b + 1], 0.0, ALU.mult, ALU.add)
+            nc.gpsimd.tensor_scalar(kept[:], hx_sb[:, b, :], one_minus_cm[:, b : b + 1], 0.0, ALU.mult, ALU.add)
 
-            m_r = mixed("m_r", pieces, 0)
+            m_z, m_r = mixed(pieces, ("z", "r"))
+            z = work.tile([P, N], F32, name="z")
+            nc.scalar.activation(z[:], m_z[:], FUNC.Sigmoid, bias=bias_rz[:, 2 + b : 3 + b])
+            share_n = work.tile([P, N], F32, name="share_n")
+            nc.gpsimd.tensor_scalar(share_n[:], z[:], neg_cm[:, b : b + 1], cm, ALU.mult, ALU.add)
+            share_h = work.tile([P, N], F32, name="share_h")
+            nc.gpsimd.tensor_tensor(share_h[:], masked_h[:], z[:], ALU.mult)
+
             r = work.tile([P, N], F32, name="r")
-            nc.scalar.activation(r[:], m_r[:], FUNC.Sigmoid, bias=bias_r[:, b : b + 1])
-
-            m_hn = mixed("m_hn", pieces, 2)
+            nc.scalar.activation(r[:], m_r[:], FUNC.Sigmoid, bias=bias_rz[:, b : b + 1])
+            (m_hn,) = mixed(pieces, ("hn",))
             r_hn = work.tile([P, N], F32, name="r_hn")
             nc.vector.scalar_tensor_tensor(
                 r_hn[:], m_hn[:], cols[:, 10 + b : 11 + b], r[:], ALU.add, ALU.mult
             )
-            m_in = mixed("m_in", pieces, 3)
+            (m_in,) = mixed(pieces, ("in",))
             pre_n = work.tile([P, N], F32, name="pre_n")
-            nc.vector.tensor_tensor(pre_n[:], r_hn[:], m_in[:], ALU.add)
             n = work.tile([P, N], F32, name="n")
-            nc.scalar.activation(n[:], pre_n[:], FUNC.Tanh, bias=cols[:, 4 + b : 5 + b])
-
-            gap = work.tile([P, N], F32, name="gap")
-            nc.vector.scalar_tensor_tensor(gap[:], n[:], cm, masked_h[:], ALU.mult, ALU.subtract)
-            m_z = mixed("m_z", pieces, 1)
-            one_minus_z = work.tile([P, N], F32, name="one_minus_z")
-            nc.scalar.activation(
-                one_minus_z[:], m_z[:], FUNC.Sigmoid, bias=neg_bias_z[:, b : b + 1], scale=-1.0
-            )
+            new_part = work.tile([P, N], F32, name="new_part")
+            renewed = work.tile([P, N], F32, name="renewed")
+            halves = [slice(0, N // 2), slice(N // 2, N)]
+            for half in halves:
+                nc.vector.tensor_tensor(pre_n[:, half], r_hn[:, half], m_in[:, half], ALU.add)
+                nc.scalar.activation(n[:, half], pre_n[:, half], FUNC.Tanh, bias=cols[:, 4 + b : 5 + b])
             if b + 1 < BLOCKS:
                 pieces = project(b + 1)
-
-            moved = work.tile([P, N], F32, name="moved")
-            nc.vector.tensor_tensor(moved[:], gap[:], one_minus_z[:], ALU.mult)
-            renewed = work.tile([P, N], F32, name="renewed")
-            nc.vector.tensor_tensor(renewed[:], moved[:], masked_h[:], ALU.add)
+            for half in halves:
+                nc.vector.tensor_tensor(new_part[:, half], n[:, half], share_n[:, half], ALU.mult)
+            for half in halves:
+                nc.vector.tensor_tensor(renewed[:, half], new_part[:, half], share_h[:, half], ALU.add)
 
             nc.vector.tensor_tensor(window[b][:].indirect(offsets[:]), renewed[:], kept[:], ALU.add)
             nc.sync.dma_start(out[b * P : (b + 1) * P, :], window[b][:])

@@ -143,18 +143,15 @@ def tile_staticgraphgrucell_kernel(
 
         for b in range(BLOCKS):
             cm = cols[:, 12 + b : 13 + b]
-            masked_h = work.tile([P, N], F32, name="masked_h")
-            nc.gpsimd.tensor_scalar(masked_h[:], hx_sb[:, b, :], cm, 0.0, ALU.mult, ALU.add)
-            kept = work.tile([P, N], F32, name="kept")
-            nc.gpsimd.tensor_scalar(kept[:], hx_sb[:, b, :], one_minus_cm[:, b : b + 1], 0.0, ALU.mult, ALU.add)
-
             m_z, m_r = mixed(pieces, ("z", "r"))
             z = work.tile([P, N], F32, name="z")
             nc.scalar.activation(z[:], m_z[:], FUNC.Sigmoid, bias=bias_rz[:, 2 + b : 3 + b])
             share_n = work.tile([P, N], F32, name="share_n")
             nc.gpsimd.tensor_scalar(share_n[:], z[:], neg_cm[:, b : b + 1], cm, ALU.mult, ALU.add)
             share_h = work.tile([P, N], F32, name="share_h")
-            nc.gpsimd.tensor_tensor(share_h[:], masked_h[:], z[:], ALU.mult)
+            nc.gpsimd.tensor_scalar(share_h[:], z[:], cm, one_minus_cm[:, b : b + 1], ALU.mult, ALU.add)
+            old_part = work.tile([P, N], F32, name="old_part")
+            nc.gpsimd.tensor_tensor(old_part[:], share_h[:], hx_sb[:, b, :], ALU.mult)
 
             r = work.tile([P, N], F32, name="r")
             nc.scalar.activation(r[:], m_r[:], FUNC.Sigmoid, bias=bias_rz[:, b : b + 1])
@@ -167,7 +164,6 @@ def tile_staticgraphgrucell_kernel(
             pre_n = work.tile([P, N], F32, name="pre_n")
             n = work.tile([P, N], F32, name="n")
             new_part = work.tile([P, N], F32, name="new_part")
-            renewed = work.tile([P, N], F32, name="renewed")
             halves = [slice(0, N // 2), slice(N // 2, N)]
             for half in halves:
                 nc.vector.tensor_tensor(pre_n[:, half], r_hn[:, half], m_in[:, half], ALU.add)
@@ -176,8 +172,6 @@ def tile_staticgraphgrucell_kernel(
                 pieces = project(b + 1)
             for half in halves:
                 nc.vector.tensor_tensor(new_part[:, half], n[:, half], share_n[:, half], ALU.mult)
-            for half in halves:
-                nc.vector.tensor_tensor(renewed[:, half], new_part[:, half], share_h[:, half], ALU.add)
 
-            nc.vector.tensor_tensor(window[b][:].indirect(offsets[:]), renewed[:], kept[:], ALU.add)
+            nc.vector.tensor_tensor(window[b][:].indirect(offsets[:]), new_part[:], old_part[:], ALU.add)
             nc.sync.dma_start(out[b * P : (b + 1) * P, :], window[b][:])

@@ -18,6 +18,7 @@ GROUP = P // NODES
 WARM_UP = 4
 QUARTER = {"r": 0, "z": 1, "hn": 2, "in": 3}
 ROWS = 14
+CHAIN_PARTS = 4
 
 FLOPS = 2 * (D + H) * GATES * H * N + 2 * NODES * 2 * GATES * H * N
 
@@ -156,22 +157,23 @@ def tile_staticgraphgrucell_kernel(
             r = work.tile([P, N], F32, name="r")
             nc.scalar.activation(r[:], m_r[:], FUNC.Sigmoid, bias=bias_rz[:, b : b + 1])
             (m_hn,) = mixed(pieces, ("hn",))
+            parts = [slice(i * N // CHAIN_PARTS, (i + 1) * N // CHAIN_PARTS) for i in range(CHAIN_PARTS)]
             r_hn = work.tile([P, N], F32, name="r_hn")
-            nc.vector.scalar_tensor_tensor(
-                r_hn[:], m_hn[:], cols[:, 10 + b : 11 + b], r[:], ALU.add, ALU.mult
-            )
+            for part in parts:
+                nc.vector.scalar_tensor_tensor(
+                    r_hn[:, part], m_hn[:, part], cols[:, 10 + b : 11 + b], r[:, part], ALU.add, ALU.mult
+                )
             (m_in,) = mixed(pieces, ("in",))
             pre_n = work.tile([P, N], F32, name="pre_n")
             n = work.tile([P, N], F32, name="n")
             new_part = work.tile([P, N], F32, name="new_part")
-            halves = [slice(0, N // 2), slice(N // 2, N)]
-            for half in halves:
-                nc.vector.tensor_tensor(pre_n[:, half], r_hn[:, half], m_in[:, half], ALU.add)
-                nc.scalar.activation(n[:, half], pre_n[:, half], FUNC.Tanh, bias=cols[:, 4 + b : 5 + b])
+            for part in parts:
+                nc.vector.tensor_tensor(pre_n[:, part], r_hn[:, part], m_in[:, part], ALU.add)
+                nc.scalar.activation(n[:, part], pre_n[:, part], FUNC.Tanh, bias=cols[:, 4 + b : 5 + b])
             if b + 1 < BLOCKS:
                 pieces = project(b + 1)
-            for half in halves:
-                nc.vector.tensor_tensor(new_part[:, half], n[:, half], share_n[:, half], ALU.mult)
+            for part in parts:
+                nc.vector.tensor_tensor(new_part[:, part], n[:, part], share_n[:, part], ALU.mult)
 
             nc.vector.tensor_tensor(window[b][:].indirect(offsets[:]), new_part[:], old_part[:], ALU.add)
             nc.sync.dma_start(out[b * P : (b + 1) * P, :], window[b][:])

@@ -147,15 +147,14 @@ def tile_staticgraphgrucell_kernel(
             m_z, m_r = mixed(pieces, ("z", "r"))
             z = work.tile([P, N], F32, name="z")
             nc.scalar.activation(z[:], m_z[:], FUNC.Sigmoid, bias=bias_rz[:, 2 + b : 3 + b])
-            share_n = work.tile([P, N], F32, name="share_n")
-            nc.gpsimd.tensor_scalar(share_n[:], z[:], neg_cm[:, b : b + 1], cm, ALU.mult, ALU.add)
-            share_h = work.tile([P, N], F32, name="share_h")
-            nc.gpsimd.tensor_scalar(share_h[:], z[:], cm, one_minus_cm[:, b : b + 1], ALU.mult, ALU.add)
-            old_part = work.tile([P, N], F32, name="old_part")
-            nc.gpsimd.tensor_tensor(old_part[:], share_h[:], hx_sb[:, b, :], ALU.mult)
-
             r = work.tile([P, N], F32, name="r")
             nc.scalar.activation(r[:], m_r[:], FUNC.Sigmoid, bias=bias_rz[:, b : b + 1])
+            share_h = work.tile([P, N], F32, name="share_h")
+            nc.scalar.activation(share_h[:], z[:], FUNC.Identity, bias=one_minus_cm[:, b : b + 1], scale=cm)
+            old_part = work.tile([P, N], F32, name="old_part")
+            nc.gpsimd.tensor_tensor(old_part[:], share_h[:], hx_sb[:, b, :], ALU.mult)
+            share_n = work.tile([P, N], F32, name="share_n")
+            nc.scalar.activation(share_n[:], z[:], FUNC.Identity, bias=cm, scale=neg_cm[:, b : b + 1])
             (m_hn,) = mixed(pieces, ("hn",))
             parts = [slice(i * N // CHAIN_PARTS, (i + 1) * N // CHAIN_PARTS) for i in range(CHAIN_PARTS)]
             r_hn = work.tile([P, N], F32, name="r_hn")

@@ -56,7 +56,7 @@ def tile_staticgraphgrucell_kernel(
             infl.rearrange("v u -> (v u)").partition_broadcast(P),
         )
         rows = held.tile([ROWS, P], F32, name="rows")
-        nc.gpsimd.dma_start(rows[12:14, :], cmask.rearrange("(k p) one -> k (p one)", p=P))
+        nc.scalar.dma_start(rows[12:14, :], cmask.rearrange("(k p) one -> k (p one)", p=P))
         nc.sync.dma_start(rows[0:6, :], b_ih.rearrange("(k p) one -> k (p one)", p=P))
         nc.sync.dma_start(rows[6:12, :], b_hh.rearrange("(k p) one -> k (p one)", p=P))
         offsets = held.tile([P, N // 16], U16, name="offsets")

@@ -57,8 +57,10 @@ def tile_staticgraphgrucell_kernel(
         )
         rows = held.tile([ROWS, P], F32, name="rows")
         nc.scalar.dma_start(rows[12:14, :], cmask.rearrange("(k p) one -> k (p one)", p=P))
-        nc.sync.dma_start(rows[0:6, :], b_ih.rearrange("(k p) one -> k (p one)", p=P))
-        nc.sync.dma_start(rows[6:12, :], b_hh.rearrange("(k p) one -> k (p one)", p=P))
+        for first_row, bias in ((0, b_ih), (6, b_hh)):
+            bias_rows = bias.rearrange("(k p) one -> k (p one)", p=P)
+            nc.sync.dma_start(rows[first_row : first_row + 4, :], bias_rows[0:4, :])
+            nc.sync.dma_start(rows[first_row + 4 : first_row + 6, :], bias_rows[4:6, :])
         offsets = held.tile([P, N // 16], U16, name="offsets")
         nc.sync.dma_start(offsets[:], offs)
         window = [held.tile([P, S], F32, name=f"window{b}") for b in range(BLOCKS)]

@@ -55,7 +55,8 @@ def tile_staticgraphgrucell_kernel(
             infl_sb[:].rearrange("p v u -> p (v u)"),
             infl.rearrange("v u -> (v u)").partition_broadcast(P),
         )
-        rows = held.tile([ROWS, P], F32, name="rows")
+        rows = held.tile([P, P], F32, name="rows")
+        nc.gpsimd.memset(rows[:], 0.0)
         nc.scalar.dma_start(rows[12:14, :], cmask.rearrange("(k p) one -> k (p one)", p=P))
         for first_row, bias in ((0, b_ih), (6, b_hh)):
             bias_rows = bias.rearrange("(k p) one -> k (p one)", p=P)
@@ -134,7 +135,7 @@ def tile_staticgraphgrucell_kernel(
         pieces = project(0)
 
         cols_ps = proj.tile([P, 4 * P], F32, tag="pt_ps", name="cols_ps")
-        nc.tensor.matmul(cols_ps[:, 0:ROWS], rows[:], identity[0:ROWS, 0:ROWS], start=True, stop=True)
+        nc.tensor.matmul(cols_ps[:, 0:ROWS], rows[:], identity[:, 0:ROWS], start=True, stop=True)
         cols = held.tile([P, ROWS], F32, name="cols")
         nc.vector.tensor_copy(cols[:], cols_ps[:, 0:ROWS])
         bias_rz = held.tile([P, 2 * BLOCKS], F32, name="bias_rz")

@@ -70,6 +70,10 @@ def tile_staticgraphgrucell_kernel(
         identity = held.tile([P, P], F32, name="identity")
         make_identity(nc, identity[:])
 
+        hx_f32 = held.tile([P, BLOCKS, N], F32, name="hx_f32")
+        for b in range(BLOCKS):
+            nc.gpsimd.tensor_copy(hx_f32[:, b, :], hx_sb[:, b, :])
+
         zeros = held.tile([P, N], BF16, name="zeros")
         nc.vector.memset(zeros[:], 0.0)
         idle_ps = proj.tile([P, 4 * P], F32, tag="pt_ps", name="idle_ps")
@@ -140,26 +144,16 @@ def tile_staticgraphgrucell_kernel(
         nc.vector.tensor_copy(cols[:], cols_ps[:, 0:ROWS])
         bias_rz = held.tile([P, 2 * BLOCKS], F32, name="bias_rz")
         nc.vector.tensor_tensor(bias_rz[:], cols[:, 0:4], cols[:, 6:10], ALU.add)
-        neg_cm = held.tile([P, BLOCKS], F32, name="neg_cm")
-        nc.vector.tensor_scalar(neg_cm[:], cols[:, 12:14], -1.0, None, ALU.mult)
-        one_minus_cm = held.tile([P, BLOCKS], F32, name="one_minus_cm")
-        nc.vector.tensor_scalar(one_minus_cm[:], cols[:, 12:14], -1.0, 1.0, ALU.mult, ALU.add)
+        neg_bias_z = held.tile([P, BLOCKS], F32, name="neg_bias_z")
+        nc.vector.tensor_scalar(neg_bias_z[:], bias_rz[:, 2:4], -1.0, None, ALU.mult)
 
+        parts = [slice(i * N // CHAIN_PARTS, (i + 1) * N // CHAIN_PARTS) for i in range(CHAIN_PARTS)]
         for b in range(BLOCKS):
             cm = cols[:, 12 + b : 13 + b]
-            m_z, m_r = mixed(pieces, ("z", "r"))
-            z = work.tile([P, N], F32, name="z")
-            nc.scalar.activation(z[:], m_z[:], FUNC.Sigmoid, bias=bias_rz[:, 2 + b : 3 + b])
+            (m_r,) = mixed(pieces, ("r",))
             r = work.tile([P, N], F32, name="r")
             nc.scalar.activation(r[:], m_r[:], FUNC.Sigmoid, bias=bias_rz[:, b : b + 1])
-            share_h = work.tile([P, N], F32, name="share_h")
-            nc.scalar.activation(share_h[:], z[:], FUNC.Identity, bias=one_minus_cm[:, b : b + 1], scale=cm)
-            old_part = work.tile([P, N], F32, name="old_part")
-            nc.gpsimd.tensor_tensor(old_part[:], share_h[:], hx_sb[:, b, :], ALU.mult)
-            share_n = work.tile([P, N], F32, name="share_n")
-            nc.scalar.activation(share_n[:], z[:], FUNC.Identity, bias=cm, scale=neg_cm[:, b : b + 1])
             (m_hn,) = mixed(pieces, ("hn",))
-            parts = [slice(i * N // CHAIN_PARTS, (i + 1) * N // CHAIN_PARTS) for i in range(CHAIN_PARTS)]
             r_hn = work.tile([P, N], F32, name="r_hn")
             for part in parts:
                 nc.vector.scalar_tensor_tensor(
@@ -168,14 +162,25 @@ def tile_staticgraphgrucell_kernel(
             (m_in,) = mixed(pieces, ("in",))
             pre_n = work.tile([P, N], F32, name="pre_n")
             n = work.tile([P, N], F32, name="n")
-            new_part = work.tile([P, N], F32, name="new_part")
+            step = work.tile([P, N], F32, name="step")
             for part in parts:
                 nc.vector.tensor_tensor(pre_n[:, part], r_hn[:, part], m_in[:, part], ALU.add)
                 nc.scalar.activation(n[:, part], pre_n[:, part], FUNC.Tanh, bias=cols[:, 4 + b : 5 + b])
+            (m_z,) = mixed(pieces, ("z",))
+            for part in parts:
+                nc.vector.tensor_tensor(step[:, part], n[:, part], hx_f32[:, b, part], ALU.subtract)
+            one_minus_z = work.tile([P, N], F32, name="one_minus_z")
+            change = work.tile([P, N], F32, name="change")
+            for part in parts:
+                nc.scalar.activation(
+                    one_minus_z[:, part], m_z[:, part], FUNC.Sigmoid, bias=neg_bias_z[:, b : b + 1], scale=-1.0
+                )
             if b + 1 < BLOCKS:
                 pieces = project(b + 1)
             for part in parts:
-                nc.vector.tensor_tensor(new_part[:, part], n[:, part], share_n[:, part], ALU.mult)
+                nc.vector.scalar_tensor_tensor(
+                    change[:, part], one_minus_z[:, part], cm, step[:, part], ALU.mult, ALU.mult
+                )
 
-            nc.vector.tensor_tensor(window[b][:].indirect(offsets[:]), new_part[:], old_part[:], ALU.add)
+            nc.vector.tensor_tensor(window[b][:].indirect(offsets[:]), change[:], hx_f32[:, b, :], ALU.add)
             nc.sync.dma_start(out[b * P : (b + 1) * P, :], window[b][:])

@@ -18,13 +18,23 @@ GROUP = P // NODES
 WARM_UP = 4
 QUARTER = {"r": 0, "z": 1, "hn": 2, "in": 3}
 ROWS = 14
-CHAIN_PARTS = 4
+HALVES = 2
 
 FLOPS = 2 * (D + H) * GATES * H * N + 2 * NODES * 2 * GATES * H * N
 
 
 def every_fourth(ap, s):
     return ap.rearrange("k (m s) -> k s m", s=PIECES)[:, s, :]
+
+
+def run_of_each_node(ap, i, runs):
+    return ap.rearrange("p (v i k) -> p i v k", v=NODES, i=runs)[:, i, :, :]
+
+
+def half(ap, b, i):
+    if b == 0:
+        return ap[:, i * N // HALVES : (i + 1) * N // HALVES]
+    return run_of_each_node(ap, i, HALVES)
 
 
 def gates_of_block(w, b):
@@ -41,6 +51,11 @@ def tile_staticgraphgrucell_kernel(
         tc.psum_pool(name="proj", bufs=4) as proj,
         tc.psum_pool(name="mix", bufs=1) as mix,
     ):
+        infl_sb = held.tile([P, NODES, NODES], F32, name="infl_sb")
+        nc.sync.dma_start(
+            infl_sb[:].rearrange("p v u -> p (v u)"),
+            infl.rearrange("v u -> (v u)").partition_broadcast(P),
+        )
         hx_sb = held.tile([P, BLOCKS, N], BF16, name="hx_sb")
         nc.sync.dma_start(hx_sb[:], hx.rearrange("(k p) j -> p k j", p=P))
         w_hh_sb = held.tile([P, BLOCKS, GATES * H], BF16, name="w_hh_sb")
@@ -50,11 +65,6 @@ def tile_staticgraphgrucell_kernel(
         w_ih_sb = held.tile([D, GATES * H], BF16, name="w_ih_sb")
         nc.scalar.dma_start(w_ih_sb[:], w_ih)
 
-        infl_sb = held.tile([P, NODES, NODES], F32, name="infl_sb")
-        nc.sync.dma_start(
-            infl_sb[:].rearrange("p v u -> p (v u)"),
-            infl.rearrange("v u -> (v u)").partition_broadcast(P),
-        )
         rows = held.tile([P, P], F32, name="rows")
         nc.gpsimd.memset(rows[:], 0.0)
         nc.scalar.dma_start(rows[12:14, :], cmask.rearrange("(k p) one -> k (p one)", p=P))
@@ -73,6 +83,13 @@ def tile_staticgraphgrucell_kernel(
         hx_f32 = held.tile([P, BLOCKS, N], F32, name="hx_f32")
         for b in range(BLOCKS):
             nc.gpsimd.tensor_copy(hx_f32[:, b, :], hx_sb[:, b, :])
+        hx_runs = held.tile([P, BLOCKS, N], BF16, name="hx_runs")
+        x_runs = held.tile([D, N], BF16, name="x_runs")
+        for runs, straight in ((hx_runs[:, 0, :], hx_sb[:, 0, :]), (hx_runs[:, 1, :], hx_sb[:, 1, :]), (x_runs[:], x_sb[:])):
+            nc.gpsimd.tensor_copy(
+                runs.rearrange("p (s u k) -> p s u k", s=PIECES, u=NODES),
+                straight.rearrange("p (u s k) -> p s u k", s=PIECES, u=NODES),
+            )
 
         zeros = held.tile([P, N], BF16, name="zeros")
         nc.vector.memset(zeros[:], 0.0)
@@ -101,16 +118,21 @@ def tile_staticgraphgrucell_kernel(
             )
         mixer_2d = mixer[:].rearrange("p v k -> p (v k)")
 
+        def piece_columns(b, s):
+            if b == 0:
+                return every_fourth(x_sb[:], s), [every_fourth(hx_sb[:, k, :], s) for k in range(BLOCKS)]
+            part = slice(s * P, (s + 1) * P)
+            return x_runs[:, part], [hx_runs[:, k, part] for k in range(BLOCKS)]
+
         def project(b):
             pieces = []
             for s in range(PIECES):
-                x_s = every_fourth(x_sb[:], s)
+                x_s, hx_s = piece_columns(b, s)
                 pt_ps = proj.tile([P, 4 * P], F32, name="pt_ps")
                 r_z_hn = pt_ps[:, 0 : 3 * P].rearrange("m (g c) -> m g c", g=GATES)
                 for k in range(BLOCKS):
                     nc.tensor.matmul(
-                        r_z_hn, every_fourth(hx_sb[:, k, :], s), gates_of_block(w_hh_sb[:, k, :], b),
-                        start=(k == 0), stop=False,
+                        r_z_hn, hx_s[k], gates_of_block(w_hh_sb[:, k, :], b), start=(k == 0), stop=False
                     )
                 nc.tensor.matmul(
                     r_z_hn[:, 0:2, :], x_s, gates_of_block(w_ih_sb[:], b)[:, 0:2, :], start=False, stop=True
@@ -119,22 +141,25 @@ def tile_staticgraphgrucell_kernel(
                     pt_ps[:, 3 * P : 4 * P], x_s, gates_of_block(w_ih_sb[:], b)[:, 2, :], start=True, stop=True
                 )
                 pt_sb = held.tile([P, 4 * P], F32, name=f"pt_sb{b}{s}")
-                if b == 0 and s % 2 == 1:
-                    nc.vector.tensor_copy(pt_sb[:], pt_ps[:])
-                else:
-                    nc.scalar.copy(pt_sb[:], pt_ps[:])
+                nc.scalar.copy(pt_sb[:], pt_ps[:])
                 pieces.append(pt_sb)
             return pieces
 
-        def mixed(pieces, quarters):
-            m_ps = [mix.tile([P, N], F32, tag=f"m_{q}", name=f"m_{q}") for q in quarters]
+        def mixed(b, pieces, quarter, banks):
+            first = QUARTER[quarter] * P
+            m_ps = [pool.tile([P, N], F32, tag=tag, name="m_ps") for pool, tag in banks]
             for s in range(PIECES):
-                for m, q in zip(m_ps, quarters):
-                    first = QUARTER[q] * P
-                    nc.tensor.matmul(
-                        every_fourth(m[:], s), pieces[s][:, first : first + P], mixer_2d, start=True, stop=True
-                    )
-            return m_ps
+                if b == 0:
+                    out_s, mixer_s = every_fourth(m_ps[0][:], s), mixer_2d
+                elif len(banks) == 1:
+                    out_s, mixer_s = run_of_each_node(m_ps[0][:], s, PIECES), mixer[:]
+                else:
+                    bank = m_ps[s // 2][:, 0 : N // HALVES]
+                    out_s, mixer_s = run_of_each_node(bank, s % 2, PIECES // HALVES), mixer[:]
+                nc.tensor.matmul(out_s, pieces[s][:, first : first + P], mixer_s, start=True, stop=True)
+            if len(banks) == 1:
+                return [half(m_ps[0][:], b, i) for i in range(HALVES)]
+            return [m[:, 0 : N // HALVES].rearrange("p (v k) -> p v k", v=NODES) for m in m_ps]
 
         pieces = project(0)
 
@@ -147,39 +172,40 @@ def tile_staticgraphgrucell_kernel(
         neg_bias_z = held.tile([P, BLOCKS], F32, name="neg_bias_z")
         nc.vector.tensor_scalar(neg_bias_z[:], bias_rz[:, 2:4], -1.0, None, ALU.mult)
 
-        parts = [slice(i * N // CHAIN_PARTS, (i + 1) * N // CHAIN_PARTS) for i in range(CHAIN_PARTS)]
+        banks = {
+            (0, "r"): [(mix, "m_r")], (0, "hn"): [(mix, "m_hn")], (0, "in"): [(mix, "m_in")], (0, "z"): [(mix, "m_z")],
+            (1, "r"): [(mix, "m_r")], (1, "hn"): [(mix, "m_hn")],
+            (1, "in"): [(mix, "m_in"), (mix, "m_z")], (1, "z"): [(proj, "pt_ps"), (proj, "pt_ps")],
+        }
         for b in range(BLOCKS):
             cm = cols[:, 12 + b : 13 + b]
-            (m_r,) = mixed(pieces, ("r",))
-            r = work.tile([P, N], F32, name="r")
-            nc.scalar.activation(r[:], m_r[:], FUNC.Sigmoid, bias=bias_rz[:, b : b + 1])
-            (m_hn,) = mixed(pieces, ("hn",))
-            r_hn = work.tile([P, N], F32, name="r_hn")
-            for part in parts:
+            r, r_hn, pre_n, n, step, one_minus_z, change = (
+                work.tile([P, N], F32, name=name) for name in ("r", "r_hn", "pre_n", "n", "step", "one_minus_z", "change")
+            )
+            m_r = mixed(b, pieces, "r", banks[b, "r"])
+            for i in range(HALVES):
+                nc.scalar.activation(half(r[:], b, i), m_r[i], FUNC.Sigmoid, bias=bias_rz[:, b : b + 1])
+            m_hn = mixed(b, pieces, "hn", banks[b, "hn"])
+            for i in range(HALVES):
                 nc.vector.scalar_tensor_tensor(
-                    r_hn[:, part], m_hn[:, part], cols[:, 10 + b : 11 + b], r[:, part], ALU.add, ALU.mult
+                    half(r_hn[:], b, i), m_hn[i], cols[:, 10 + b : 11 + b], half(r[:], b, i), ALU.add, ALU.mult
                 )
-            (m_in,) = mixed(pieces, ("in",))
-            pre_n = work.tile([P, N], F32, name="pre_n")
-            n = work.tile([P, N], F32, name="n")
-            step = work.tile([P, N], F32, name="step")
-            for part in parts:
-                nc.vector.tensor_tensor(pre_n[:, part], r_hn[:, part], m_in[:, part], ALU.add)
-                nc.scalar.activation(n[:, part], pre_n[:, part], FUNC.Tanh, bias=cols[:, 4 + b : 5 + b])
-            (m_z,) = mixed(pieces, ("z",))
-            for part in parts:
-                nc.vector.tensor_tensor(step[:, part], n[:, part], hx_f32[:, b, part], ALU.subtract)
-            one_minus_z = work.tile([P, N], F32, name="one_minus_z")
-            change = work.tile([P, N], F32, name="change")
-            for part in parts:
+            m_in = mixed(b, pieces, "in", banks[b, "in"])
+            for i in range(HALVES):
+                nc.vector.tensor_tensor(half(pre_n[:], b, i), half(r_hn[:], b, i), m_in[i], ALU.add)
+                nc.scalar.activation(half(n[:], b, i), half(pre_n[:], b, i), FUNC.Tanh, bias=cols[:, 4 + b : 5 + b])
+            m_z = mixed(b, pieces, "z", banks[b, "z"])
+            for i in range(HALVES):
+                nc.vector.tensor_tensor(half(step[:], b, i), half(n[:], b, i), half(hx_f32[:, b, :], b, i), ALU.subtract)
+            for i in range(HALVES):
                 nc.scalar.activation(
-                    one_minus_z[:, part], m_z[:, part], FUNC.Sigmoid, bias=neg_bias_z[:, b : b + 1], scale=-1.0
+                    half(one_minus_z[:], b, i), m_z[i], FUNC.Sigmoid, bias=neg_bias_z[:, b : b + 1], scale=-1.0
                 )
             if b + 1 < BLOCKS:
                 pieces = project(b + 1)
-            for part in parts:
+            for i in range(HALVES):
                 nc.vector.scalar_tensor_tensor(
-                    change[:, part], one_minus_z[:, part], cm, step[:, part], ALU.mult, ALU.mult
+                    half(change[:], b, i), half(one_minus_z[:], b, i), cm, half(step[:], b, i), ALU.mult, ALU.mult
                 )
 
             nc.vector.tensor_tensor(window[b][:].indirect(offsets[:]), change[:], hx_f32[:, b, :], ALU.add)

@@ -15,7 +15,7 @@ GATES = 3
 BLOCKS = H // P
 PIECES = N // P
 GROUP = P // NODES
-WARM_UP = 4
+WARM_UP = 5
 QUARTER = {"r": 0, "z": 1, "hn": 2, "in": 3}
 ROWS = 14
 HALVES = 2
@@ -51,6 +51,9 @@ def tile_staticgraphgrucell_kernel(
         tc.psum_pool(name="proj", bufs=4) as proj,
         tc.psum_pool(name="mix", bufs=1) as mix,
     ):
+        zeros = held.tile([P, P], BF16, name="zeros")
+        nc.gpsimd.memset(zeros[:], 0.0)
+
         infl_sb = held.tile([P, NODES, NODES], F32, name="infl_sb")
         nc.sync.dma_start(
             infl_sb[:].rearrange("p v u -> p (v u)"),
@@ -91,11 +94,9 @@ def tile_staticgraphgrucell_kernel(
                 straight.rearrange("p (u s k) -> p s u k", s=PIECES, u=NODES),
             )
 
-        zeros = held.tile([P, N], BF16, name="zeros")
-        nc.vector.memset(zeros[:], 0.0)
         idle_ps = proj.tile([P, 4 * P], F32, tag="pt_ps", name="idle_ps")
         for i in range(WARM_UP):
-            nc.tensor.matmul(idle_ps[:], zeros[:, 0:P], zeros[:], start=True, stop=True)
+            nc.tensor.matmul(idle_ps[:], zeros[:], zeros[:, 0:1].to_broadcast([P, N]), start=True, stop=True)
         idle_sb = held.tile([P, 1], F32, name="idle_sb")
         nc.scalar.activation(idle_sb[:], zeros[:, 0:1], FUNC.Sigmoid)
 

import concourse.mybir as mybir
from concourse.masks import make_identity

F32 = mybir.dt.float32
BF16 = mybir.dt.bfloat16
U16 = mybir.dt.uint16
ALU = mybir.AluOpType
FUNC = mybir.ActivationFunctionType

P = 128
H, D = 256, 128
S, N = 4096, 512
NODES = 4
GATES = 3
BLOCKS = H // P
PIECES = N // P
GROUP = P // NODES
WARM_UP = 5
QUARTER = {"r": 0, "z": 1, "hn": 2, "in": 3}
ROWS = 14
HALVES = 2

FLOPS = 2 * (D + H) * GATES * H * N + 2 * NODES * 2 * GATES * H * N


def every_fourth(ap, s):
    return ap.rearrange("k (m s) -> k s m", s=PIECES)[:, s, :]


def run_of_each_node(ap, i, runs):
    return ap.rearrange("p (v i k) -> p i v k", v=NODES, i=runs)[:, i, :, :]


def half(ap, b, i):
    if b == 0:
        return ap[:, i * N // HALVES : (i + 1) * N // HALVES]
    return run_of_each_node(ap, i, HALVES)


def gates_of_block(w, b):
    return w.rearrange("k (g b c) -> k b g c", g=GATES, b=BLOCKS)[:, b, :, :]


def tile_staticgraphgrucell_kernel(
    tc, base, x, hx, w_ih, w_hh, b_ih, b_hh, infl, cmask, offs, out
):
    nc = tc.nc
    with (
        tc.tile_pool(name="held", bufs=1) as held,
        tc.tile_pool(name="work", bufs=2) as work,
        tc.psum_pool(name="proj", bufs=4) as proj,
        tc.psum_pool(name="mix", bufs=1) as mix,
    ):
        zeros = held.tile([P, P], BF16, name="zeros")
        nc.gpsimd.memset(zeros[:], 0.0)

        infl_sb = held.tile([P, NODES, NODES], F32, name="infl_sb")
        nc.sync.dma_start(
            infl_sb[:].rearrange("p v u -> p (v u)"),
            infl.rearrange("v u -> (v u)").partition_broadcast(P),
        )
        hx_sb = held.tile([P, BLOCKS, N], BF16, name="hx_sb")
        nc.sync.dma_start(hx_sb[:], hx.rearrange("(k p) j -> p k j", p=P))
        w_hh_sb = held.tile([P, BLOCKS, GATES * H], BF16, name="w_hh_sb")
        nc.scalar.dma_start(w_hh_sb[:], w_hh.rearrange("(k p) o -> p k o", p=P))
        x_sb = held.tile([D, N], BF16, name="x_sb")
        nc.sync.dma_start(x_sb[:], x)
        w_ih_sb = held.tile([D, GATES * H], BF16, name="w_ih_sb")
        nc.scalar.dma_start(w_ih_sb[:], w_ih)

        rows = held.tile([P, P], F32, name="rows")
        nc.gpsimd.memset(rows[:], 0.0)
        nc.scalar.dma_start(rows[12:14, :], cmask.rearrange("(k p) one -> k (p one)", p=P))
        for first_row, bias in ((0, b_ih), (6, b_hh)):
            bias_rows = bias.rearrange("(k p) one -> k (p one)", p=P)
            nc.sync.dma_start(rows[first_row : first_row + 4, :], bias_rows[0:4, :])
            nc.sync.dma_start(rows[first_row + 4 : first_row + 6, :], bias_rows[4:6, :])
        offsets = held.tile([P, N // 16], U16, name="offsets")
        nc.sync.dma_start(offsets[:], offs)
        window = [held.tile([P, S], F32, name=f"window{b}") for b in range(BLOCKS)]
        for b in range(BLOCKS):
            nc.sync.dma_start(window[b][:], base[b * P : (b + 1) * P, :])
        identity = held.tile([P, P], F32, name="identity")
        make_identity(nc, identity[:])

        hx_f32 = held.tile([P, BLOCKS, N], F32, name="hx_f32")
        for b in range(BLOCKS):
            nc.gpsimd.tensor_copy(hx_f32[:, b, :], hx_sb[:, b, :])
        hx_runs = held.tile([P, BLOCKS, N], BF16, name="hx_runs")
        x_runs = held.tile([D, N], BF16, name="x_runs")
        for runs, straight in ((hx_runs[:, 0, :], hx_sb[:, 0, :]), (hx_runs[:, 1, :], hx_sb[:, 1, :]), (x_runs[:], x_sb[:])):
            nc.gpsimd.tensor_copy(
                runs.rearrange("p (s u k) -> p s u k", s=PIECES, u=NODES),
                straight.rearrange("p (u s k) -> p s u k", s=PIECES, u=NODES),
            )

        idle_ps = proj.tile([P, 4 * P], F32, tag="pt_ps", name="idle_ps")
        for i in range(WARM_UP):
            nc.tensor.matmul(idle_ps[:], zeros[:], zeros[:, 0:1].to_broadcast([P, N]), start=True, stop=True)
        idle_sb = held.tile([P, 1], F32, name="idle_sb")
        nc.scalar.activation(idle_sb[:], zeros[:, 0:1], FUNC.Sigmoid)

        row_sum = held.tile([P, NODES], F32, name="row_sum")
        nc.vector.reduce_sum(row_sum[:], infl_sb[:], axis=mybir.AxisListType.X)
        row_inv = held.tile([P, NODES], F32, name="row_inv")
        nc.vector.reciprocal(row_inv[:], row_sum[:])
        a_sb = held.tile([P, NODES, NODES], F32, name="a_sb")
        nc.vector.tensor_tensor(
            a_sb[:], infl_sb[:], row_inv[:].unsqueeze(2).to_broadcast([P, NODES, NODES]), ALU.mult
        )
        mixer = held.tile([P, NODES, GROUP], F32, name="mixer")
        for u in range(NODES):
            part = slice(u * GROUP, (u + 1) * GROUP)
            nc.vector.tensor_tensor(
                mixer[part, :, :],
                identity[part, part].unsqueeze(1).to_broadcast([GROUP, NODES, GROUP]),
                a_sb[part, :, u : u + 1].to_broadcast([GROUP, NODES, GROUP]),
                ALU.mult,
            )
        mixer_2d = mixer[:].rearrange("p v k -> p (v k)")

        def piece_columns(b, s):
            if b == 0:
                return every_fourth(x_sb[:], s), [every_fourth(hx_sb[:, k, :], s) for k in range(BLOCKS)]
            part = slice(s * P, (s + 1) * P)
            return x_runs[:, part], [hx_runs[:, k, part] for k in range(BLOCKS)]

        def project(b):
            pieces = []
            for s in range(PIECES):
                x_s, hx_s = piece_columns(b, s)
                pt_ps = proj.tile([P, 4 * P], F32, name="pt_ps")
                r_z_hn = pt_ps[:, 0 : 3 * P].rearrange("m (g c) -> m g c", g=GATES)
                for k in range(BLOCKS):
                    nc.tensor.matmul(
                        r_z_hn, hx_s[k], gates_of_block(w_hh_sb[:, k, :], b), start=(k == 0), stop=False
                    )
                nc.tensor.matmul(
                    r_z_hn[:, 0:2, :], x_s, gates_of_block(w_ih_sb[:], b)[:, 0:2, :], start=False, stop=True
                )
                nc.tensor.matmul(
                    pt_ps[:, 3 * P : 4 * P], x_s, gates_of_block(w_ih_sb[:], b)[:, 2, :], start=True, stop=True
                )
                pt_sb = held.tile([P, 4 * P], F32, name=f"pt_sb{b}{s}")
                nc.scalar.copy(pt_sb[:], pt_ps[:])
                pieces.append(pt_sb)
            return pieces

        def mixed(b, pieces, quarter, banks):
            first = QUARTER[quarter] * P
            m_ps = [pool.tile([P, N], F32, tag=tag, name="m_ps") for pool, tag in banks]
            for s in range(PIECES):
                if b == 0:
                    out_s, mixer_s = every_fourth(m_ps[0][:], s), mixer_2d
                elif len(banks) == 1:
                    out_s, mixer_s = run_of_each_node(m_ps[0][:], s, PIECES), mixer[:]
                else:
                    bank = m_ps[s // 2][:, 0 : N // HALVES]
                    out_s, mixer_s = run_of_each_node(bank, s % 2, PIECES // HALVES), mixer[:]
                nc.tensor.matmul(out_s, pieces[s][:, first : first + P], mixer_s, start=True, stop=True)
            if len(banks) == 1:
                return [half(m_ps[0][:], b, i) for i in range(HALVES)]
            return [m[:, 0 : N // HALVES].rearrange("p (v k) -> p v k", v=NODES) for m in m_ps]

        pieces = project(0)

        cols_ps = proj.tile([P, 4 * P], F32, tag="pt_ps", name="cols_ps")
        nc.tensor.matmul(cols_ps[:, 0:ROWS], rows[:], identity[:, 0:ROWS], start=True, stop=True)
        cols = held.tile([P, ROWS], F32, name="cols")
        nc.vector.tensor_copy(cols[:], cols_ps[:, 0:ROWS])
        bias_rz = held.tile([P, 2 * BLOCKS], F32, name="bias_rz")
        nc.vector.tensor_tensor(bias_rz[:], cols[:, 0:4], cols[:, 6:10], ALU.add)
        neg_bias_z = held.tile([P, BLOCKS], F32, name="neg_bias_z")
        nc.vector.tensor_scalar(neg_bias_z[:], bias_rz[:, 2:4], -1.0, None, ALU.mult)

        banks = {
            (0, "r"): [(mix, "m_r")], (0, "hn"): [(mix, "m_hn")], (0, "in"): [(mix, "m_in")], (0, "z"): [(mix, "m_z")],
            (1, "r"): [(mix, "m_r")], (1, "hn"): [(mix, "m_hn")],
            (1, "in"): [(mix, "m_in"), (mix, "m_z")], (1, "z"): [(proj, "pt_ps"), (proj, "pt_ps")],
        }
        for b in range(BLOCKS):
            cm = cols[:, 12 + b : 13 + b]
            r, r_hn, pre_n, n, step, one_minus_z, change = (
                work.tile([P, N], F32, name=name) for name in ("r", "r_hn", "pre_n", "n", "step", "one_minus_z", "change")
            )
            m_r = mixed(b, pieces, "r", banks[b, "r"])
            for i in range(HALVES):
                nc.scalar.activation(half(r[:], b, i), m_r[i], FUNC.Sigmoid, bias=bias_rz[:, b : b + 1])
            m_hn = mixed(b, pieces, "hn", banks[b, "hn"])
            for i in range(HALVES):
                nc.vector.scalar_tensor_tensor(
                    half(r_hn[:], b, i), m_hn[i], cols[:, 10 + b : 11 + b], half(r[:], b, i), ALU.add, ALU.mult
                )
            m_in = mixed(b, pieces, "in", banks[b, "in"])
            for i in range(HALVES):
                nc.vector.tensor_tensor(half(pre_n[:], b, i), half(r_hn[:], b, i), m_in[i], ALU.add)
                nc.scalar.activation(half(n[:], b, i), half(pre_n[:], b, i), FUNC.Tanh, bias=cols[:, 4 + b : 5 + b])
            m_z = mixed(b, pieces, "z", banks[b, "z"])
            for i in range(HALVES):
                nc.vector.tensor_tensor(half(step[:], b, i), half(n[:], b, i), half(hx_f32[:, b, :], b, i), ALU.subtract)
            for i in range(HALVES):
                nc.scalar.activation(
                    half(one_minus_z[:], b, i), m_z[i], FUNC.Sigmoid, bias=neg_bias_z[:, b : b + 1], scale=-1.0
                )
            if b + 1 < BLOCKS:
                pieces = project(b + 1)
            for i in range(HALVES):
                nc.vector.scalar_tensor_tensor(
                    half(change[:], b, i), half(one_minus_z[:], b, i), cm, half(step[:], b, i), ALU.mult, ALU.mult
                )

            nc.vector.tensor_tensor(window[b][:].indirect(offsets[:]), change[:], hx_f32[:, b, :], ALU.add)
            nc.sync.dma_start(out[b * P : (b + 1) * P, :], window[b][:])
